import numpy as np
import ml_dtypes


def mxq(x, axis, fmt="e4m3"):
    dtype, down = {"e4m3": (ml_dtypes.float8_e4m3fn, 7), "e5m2": (ml_dtypes.float8_e5m2, 14)}[fmt]
    v = np.moveaxis(np.asarray(x, np.float32).astype(ml_dtypes.bfloat16).astype(np.float64), axis, -1)
    blocks = v.reshape(v.shape[:-1] + (-1, 32))
    amax = np.abs(blocks).max(-1, keepdims=True)
    byte = np.maximum(np.where(amax > 0, np.frexp(amax)[1] - 1 + 127, 0) - down, 1)
    scale = np.exp2(byte - 127.0)
    codes = (blocks / scale).astype(np.float32).astype(dtype).astype(np.float64)
    return np.moveaxis((codes * scale).reshape(v.shape), -1, axis)


WIDE = False


def mx_kscale(k):
    if not WIDE:
        return np.ones(k)
    levels = np.array([10, -10, 5, -5, 0])
    if k % 512:
        return np.exp2(np.random.permutation(np.resize(levels, k // 32))).repeat(32)
    a = np.empty((k // 512, 16))
    for p in range(k // 512):
        a[p, :8] = np.random.permutation(np.resize(levels, 8))
        for g in range(8):
            far = levels[np.abs(levels - a[p, g]) >= 10]
            a[p, g + 8] = far[np.random.randint(len(far))]
    return np.exp2(a.ravel()).repeat(32)


BF16 = ml_dtypes.bfloat16


def bf(x):
    return np.asarray(x, np.float32).astype(BF16)


def f64(x):
    return np.asarray(x).astype(np.float64)


B, K, NH, N = 256, 1024, 512, 512
EPSILON = 0.1


def setup_inputs():
    s = mx_kscale(K)
    g = 1.0 / np.mean(1.0 / s)
    return {"x": bf(np.random.standard_normal((B, K)) * s),
            "y": bf(np.random.standard_normal((B, N)) * 12.0 / np.sqrt(K) * g),
            "beta": bf(np.random.random((K, N)) * 1.7 / np.sqrt(K) / s[:, None]),
            "bias_lin": bf(np.random.standard_normal(N) * 0.1),
            "W1": bf(-np.random.random((NH, K)) * 1.7 / np.sqrt(K) / s[None, :]),
            "W2": bf(np.random.random((N, NH)) * (0.5 + np.random.random((N, 1))) * 2.0 / NH**2),
            "bias1": bf(np.random.standard_normal(NH) * 0.1),
            "bias2": bf(np.random.standard_normal(N) * 0.1),
            "adv": 1}


def reference(x, y, beta, bias_lin, W1, W2, bias1, bias2, adv):
    xq = mxq(f64(x), 1, "e4m3")
    lin = (xq @ mxq(f64(beta), 0, "e4m3")) + f64(bias_lin)
    if adv:
        beta_norm = np.sum(np.abs(f64(beta)), axis=0)
        lin = lin - EPSILON * f64(y) * beta_norm
    if adv:
        one = NH * np.sum(f64(W2), axis=1) + f64(bias2)
        one = np.broadcast_to(one, lin.shape)
    else:
        h = np.maximum((xq @ mxq(f64(W1), 1, "e4m3").T) + f64(bias1), 0.0)
        one = (mxq(h, 1, "e4m3") @ mxq(f64(W2), 1, "e4m3").T) + f64(bias2)
    return lin + one

@@ -1,0 +1,195 @@
+from contextlib import ExitStack
+
+import concourse.mybir as mybir
+from concourse.masks import make_identity
+
+F32 = mybir.dt.float32
+BF16 = mybir.dt.bfloat16
+U32 = mybir.dt.uint32
+U8 = mybir.dt.uint8
+FP8X4 = mybir.dt.float8_e4m3fn_x4
+ALU = mybir.AluOpType
+ACT = mybir.ActivationFunctionType
+AXIS = mybir.AxisListType
+
+P = 128
+PACK = 4
+K_PASS = P * PACK
+B, K, N, NH = 256, 1024, 512, 512
+PASSES = K // K_PASS
+ROW_TILES = B // P
+COL_TILES = N // P
+EPSILON = 0.1
+
+VECTOR_COLS = 256
+
+FLOPS = 2 * B * K * N
+BYTES = 2 * (B * K + B * N + K * N + N * NH + 2 * N) + 4 * B * N
+
+
+def tile_advresnet_s_kernel(tc, x, y, beta, bias_lin, W1, W2, bias1, bias2, adv, out):
+    assert adv == 1
+    nc = tc.nc
+    with ExitStack() as ctx:
+        keep = ctx.enter_context(tc.tile_pool(name="keep", bufs=1))
+        psum = ctx.enter_context(tc.psum_pool(name="psum", bufs=1))
+        ctx.enter_context(tc.manual_schedule())
+
+        beta_sb = keep.tile([P, PASSES, PACK, N], BF16)
+        for g in range(PASSES):
+            for u in range(2):
+                rows_of_pass = beta[g * K_PASS : (g + 1) * K_PASS, :].rearrange("(p t) n -> p t n", t=PACK)
+                nc.sync.dma_start(
+                    out=beta_sb[:, g, 2 * u : 2 * u + 2, :],
+                    in_=rows_of_pass[:, 2 * u : 2 * u + 2, :],
+                )
+        x_sb = keep.tile([P, ROW_TILES * K], BF16)
+        nc.sync.dma_start(
+            out=x_sb[:].rearrange("p (r k) -> p r k", r=ROW_TILES),
+            in_=x.rearrange("(r p) k -> p r k", p=P),
+        )
+        w2_sb = keep.tile([P, COL_TILES, NH], BF16)
+        nc.sync.dma_start(out=w2_sb[:], in_=W2.rearrange("(p t) h -> p t h", p=P))
+        y_sb = keep.tile([P, ROW_TILES, N], BF16)
+        nc.sync.dma_start(out=y_sb[:], in_=y.rearrange("(r p) n -> p r n", p=P))
+        bias_lin_sb = keep.tile([P, COL_TILES], BF16)
+        bias2_sb = keep.tile([P, COL_TILES], BF16)
+        nc.scalar.dma_start(out=bias_lin_sb[:], in_=bias_lin.rearrange("(p t) -> p t", p=P))
+        nc.scalar.dma_start(out=bias2_sb[:], in_=bias2.rearrange("(p t) -> p t", p=P))
+
+        ident = keep.tile([P, P], F32)
+        make_identity(nc, ident[:])
+        weight = keep.tile([P, 2], BF16)
+        nc.vector.memset(weight[:, 0:1], -1.0)
+        nc.vector.memset(weight[:, 1:2], 2.0)
+        table_warmer = keep.tile([P, 1], BF16)
+        nc.scalar.copy(out=table_warmer[:], in_=weight[:, 0:1])
+
+        beta_pos = keep.tile([P, PASSES, PACK, N], BF16)
+        beta_grouped = keep.tile([P, PASSES, N, PACK], BF16, align_bytes=64)
+        norm_ps = psum.tile([P, COL_TILES, 2 * PASSES], F32)
+        for g in range(PASSES):
+            for u in range(2):
+                nc.vector.tensor_scalar_max(
+                    out=beta_pos[:, g, 2 * u : 2 * u + 2, :],
+                    in0=beta_sb[:, g, 2 * u : 2 * u + 2, :],
+                    scalar1=0.0,
+                )
+            src = beta_sb[:, g].rearrange("p t (c i) -> p c t i", i=4)
+            dst = beta_grouped[:, g].rearrange("p (c i) t -> p c t i", i=4)
+            cut = VECTOR_COLS // 4
+            nc.vector.tensor_copy(out=dst[:, :cut], in_=src[:, :cut])
+            nc.scalar.copy(out=dst[:, cut:], in_=src[:, cut:])
+            for part, source in enumerate((beta_sb, beta_pos)):
+                for j in range(COL_TILES):
+                    for t in range(PACK):
+                        nc.tensor.matmul(
+                            out=norm_ps[:, j, 2 * g + part : 2 * g + part + 1],
+                            lhsT=source[:, g, t, j * P : (j + 1) * P],
+                            rhs=weight[:, part : part + 1],
+                            start=(t == 0),
+                            stop=(t == PACK - 1),
+                        )
+
+        beta_codes = keep.tile([P, PASSES, N], U32, align_bytes=64)
+        beta_scales = keep.tile([P, PASSES, N], U8, align_bytes=64)
+        norm_sb = keep.tile([P, COL_TILES], F32)
+        for g in range(PASSES):
+            nc.vector.quantize_mx(
+                out=beta_codes[:, g].bitcast(FP8X4),
+                scales=beta_scales[:, g],
+                in_=beta_grouped[:, g].rearrange("p n t -> p (n t)"),
+            )
+            if g == 0:
+                nc.vector.tensor_reduce(out=norm_sb[:], in_=norm_ps[:], axis=AXIS.X, op=ALU.add)
+
+        x_words = x_sb[:].bitcast(F32).rearrange("p (r w) -> p r w", r=ROW_TILES)
+        x_grouped = keep.tile([P, PASSES * B * PACK], BF16, align_bytes=64)
+        x_grouped_words = x_grouped[:].bitcast(F32).rearrange("p (g row u) -> p g row u", g=PASSES, u=2)
+        x_codes = keep.tile([P, PASSES * B], U32, align_bytes=64)
+        x_scales = keep.tile([P, PASSES * B], U8, align_bytes=64)
+        for g in range(PASSES):
+            xt = psum.tile([P, 2, B], F32, name="xt%d" % g)
+            for u in range(2):
+                for r in range(ROW_TILES):
+                    first_word = 2 * g * P + u
+                    nc.tensor.transpose(
+                        xt[:, u, r * P : (r + 1) * P],
+                        x_words[:, r, first_word : (g + 1) * 2 * P : 2],
+                        ident[:],
+                    )
+            if g == 0:
+                nc.scalar.copy(out=x_grouped_words[:, g], in_=xt[:].rearrange("p u row -> p row u"))
+            else:
+                nc.vector.tensor_copy(out=x_grouped_words[:, g], in_=xt[:].rearrange("p u row -> p row u"))
+        for g in range(PASSES):
+            nc.vector.quantize_mx(
+                out=x_codes[:, g * B : (g + 1) * B].bitcast(FP8X4),
+                scales=x_scales[:, g * B : (g + 1) * B],
+                in_=x_grouped[:, g * B * PACK : (g + 1) * B * PACK],
+            )
+
+        norm_rows = psum.tile([P, N], F32)
+        for j in range(COL_TILES):
+            nc.tensor.transpose(
+                norm_rows[:, j * P : (j + 1) * P],
+                norm_sb[:, j : j + 1].to_broadcast([P, P]),
+                ident[:],
+            )
+
+        acc = [psum.tile([P, N], F32, name="acc%d" % r) for r in range(ROW_TILES)]
+        for g in range(PASSES):
+            for r in range(ROW_TILES):
+                rows = slice(g * B + r * P, g * B + (r + 1) * P)
+                nc.tensor.matmul_mx(
+                    out=acc[r][:],
+                    lhsT=x_codes[:, rows].bitcast(FP8X4),
+                    lhsT_scale=x_scales[:, rows],
+                    rhs=beta_codes[:, g].bitcast(FP8X4),
+                    rhs_scale=beta_scales[:, g],
+                    start=(g == 0),
+                    stop=(g == PASSES - 1),
+                )
+
+        bias_share = keep.tile([P, COL_TILES], F32)
+        nc.gpsimd.tensor_tensor(out=bias_share[:], in0=bias_lin_sb[:], in1=bias2_sb[:], op=ALU.add)
+        nc.gpsimd.tensor_scalar(
+            out=bias_share[:], in0=bias_share[:], scalar1=1.0 / NH, scalar2=0.0, op0=ALU.mult, op1=ALU.add
+        )
+        summands = keep.tile([P, COL_TILES, NH], BF16)
+        shift_sb = keep.tile([P, COL_TILES], F32)
+        for t in range(COL_TILES):
+            nc.scalar.activation(
+                out=summands[:, t],
+                in_=w2_sb[:, t],
+                func=ACT.Identity,
+                scale=float(NH),
+                bias=bias_share[:, t : t + 1],
+                accum_out=shift_sb[:, t : t + 1],
+            )
+
+        total = keep.tile([P, ROW_TILES, N], F32)
+        for r in range(ROW_TILES):
+            nc.vector.scalar_tensor_tensor(
+                out=total[:, r],
+                in0=y_sb[:, r],
+                scalar=-EPSILON,
+                in1=norm_rows[:],
+                op0=ALU.mult,
+                op1=ALU.mult,
+            )
+        for r in range(ROW_TILES):
+            nc.vector.tensor_tensor(out=total[:, r], in0=total[:, r], in1=acc[r][:], op=ALU.add)
+        shift_rows = psum.tile([P, COL_TILES, P], F32)
+        for t in range(COL_TILES):
+            nc.tensor.transpose(
+                shift_rows[:, t, :],
+                shift_sb[:, t : t + 1].to_broadcast([P, P]),
+                ident[:],
+            )
+        for r in range(ROW_TILES):
+            total_qt = total[:, r].rearrange("p (q t) -> p q t", t=COL_TILES)
+            nc.vector.tensor_tensor(
+                out=total_qt, in0=total_qt, in1=shift_rows[:].rearrange("p t q -> p q t"), op=ALU.add
+            )
+            nc.sync.dma_start(out=out[r * P : (r + 1) * P, :], in_=total[:, r])

@@ -5,6 +5,7 @@ from concourse.masks import make_identity
 
 F32 = mybir.dt.float32
 BF16 = mybir.dt.bfloat16
+I32 = mybir.dt.int32
 U32 = mybir.dt.uint32
 U8 = mybir.dt.uint8
 FP8X4 = mybir.dt.float8_e4m3fn_x4
@@ -59,37 +60,39 @@ def tile_advresnet_s_kernel(tc, x, y, beta, bias_lin, W1, W2, bias1, bias2, adv,
 
         ident = keep.tile([P, P], F32)
         make_identity(nc, ident[:])
-        weight = keep.tile([P, 2], BF16)
-        nc.vector.memset(weight[:, 0:1], -1.0)
-        nc.vector.memset(weight[:, 1:2], 2.0)
+        ones = keep.tile([P, 1], BF16)
+        nc.vector.memset(ones[:], 1.0)
         table_warmer = keep.tile([P, 1], BF16)
-        nc.scalar.copy(out=table_warmer[:], in_=weight[:, 0:1])
+        nc.scalar.copy(out=table_warmer[:], in_=ones[:])
 
-        beta_pos = keep.tile([P, PASSES, PACK, N], BF16)
+        beta_abs = keep.tile([P, PASSES, PACK * N], BF16)
         beta_grouped = keep.tile([P, PASSES, N, PACK], BF16, align_bytes=64)
-        norm_ps = psum.tile([P, COL_TILES, 2 * PASSES], F32)
+        norm_ps = psum.tile([P, COL_TILES, PASSES], F32)
         for g in range(PASSES):
             for u in range(2):
-                nc.vector.tensor_scalar_max(
-                    out=beta_pos[:, g, 2 * u : 2 * u + 2, :],
-                    in0=beta_sb[:, g, 2 * u : 2 * u + 2, :],
-                    scalar1=0.0,
+                pair = slice(2 * u * N, (2 * u + 2) * N)
+                nc.vector.tensor_scalar(
+                    out=beta_abs[:, g, pair].bitcast(I32),
+                    in0=beta_sb[:, g].rearrange("p t n -> p (t n)")[:, pair].bitcast(I32),
+                    scalar1=0x7FFF7FFF,
+                    scalar2=None,
+                    op0=ALU.bitwise_and,
                 )
             src = beta_sb[:, g].rearrange("p t (c i) -> p c t i", i=4)
             dst = beta_grouped[:, g].rearrange("p (c i) t -> p c t i", i=4)
             cut = VECTOR_COLS // 4
             nc.vector.tensor_copy(out=dst[:, :cut], in_=src[:, :cut])
             nc.scalar.copy(out=dst[:, cut:], in_=src[:, cut:])
-            for part, source in enumerate((beta_sb, beta_pos)):
-                for j in range(COL_TILES):
-                    for t in range(PACK):
-                        nc.tensor.matmul(
-                            out=norm_ps[:, j, 2 * g + part : 2 * g + part + 1],
-                            lhsT=source[:, g, t, j * P : (j + 1) * P],
-                            rhs=weight[:, part : part + 1],
-                            start=(t == 0),
-                            stop=(t == PACK - 1),
-                        )
+            for j in range(COL_TILES):
+                for t in range(PACK):
+                    first = t * N + j * P
+                    nc.tensor.matmul(
+                        out=norm_ps[:, j, g : g + 1],
+                        lhsT=beta_abs[:, g, first : first + P],
+                        rhs=ones[:],
+                        start=(t == 0),
+                        stop=(t == PACK - 1),
+                    )
 
         beta_codes = keep.tile([P, PASSES, N], U32, align_bytes=64)
         beta_scales = keep.tile([P, PASSES, N], U8, align_bytes=64)

@@ -65,6 +65,14 @@ def tile_advresnet_s_kernel(tc, x, y, beta, bias_lin, W1, W2, bias1, bias2, adv,
         table_warmer = keep.tile([P, 1], BF16)
         nc.scalar.copy(out=table_warmer[:], in_=ones[:])
 
+        busy_ps = psum.tile([P, P], F32)
+
+        def keep_tensor_busy(count):
+            for i in range(count):
+                nc.tensor.matmul(out=busy_ps[:], lhsT=ident[:], rhs=ident[:], start=True, stop=True)
+
+        keep_tensor_busy(2)
+
         beta_abs = keep.tile([P, PASSES, PACK * N], BF16)
         beta_grouped = keep.tile([P, PASSES, N, PACK], BF16, align_bytes=64)
         norm_ps = psum.tile([P, COL_TILES, PASSES], F32)
@@ -93,6 +101,8 @@ def tile_advresnet_s_kernel(tc, x, y, beta, bias_lin, W1, W2, bias1, bias2, adv,
                         start=(t == 0),
                         stop=(t == PACK - 1),
                     )
+            if g == 0:
+                keep_tensor_busy(2)
 
         beta_codes = keep.tile([P, PASSES, N], U32, align_bytes=64)
         beta_scales = keep.tile([P, PASSES, N], U8, align_bytes=64)
@@ -125,6 +135,7 @@ def tile_advresnet_s_kernel(tc, x, y, beta, bias_lin, W1, W2, bias1, bias2, adv,
                 nc.scalar.copy(out=x_grouped_words[:, g], in_=xt[:].rearrange("p u row -> p row u"))
             else:
                 nc.vector.tensor_copy(out=x_grouped_words[:, g], in_=xt[:].rearrange("p u row -> p row u"))
+        keep_tensor_busy(2)
         for g in range(PASSES):
             nc.vector.quantize_mx(
                 out=x_codes[:, g * B : (g + 1) * B].bitcast(FP8X4),

@@ -22,7 +22,7 @@ ROW_TILES = B // P
 COL_TILES = N // P
 EPSILON = 0.1
 
-VECTOR_COLS = 256
+VECTOR_COLS = 192
 
 FLOPS = 2 * B * K * N
 BYTES = 2 * (B * K + B * N + K * N + N * NH + 2 * N) + 4 * B * N
@@ -44,15 +44,15 @@ def tile_advresnet_s_kernel(tc, x, y, beta, bias_lin, W1, W2, bias1, bias2, adv,
                     out=beta_sb[:, g, 2 * u : 2 * u + 2, :],
                     in_=rows_of_pass[:, 2 * u : 2 * u + 2, :],
                 )
-        x_sb = keep.tile([P, ROW_TILES * K], BF16)
-        nc.sync.dma_start(
-            out=x_sb[:].rearrange("p (r k) -> p r k", r=ROW_TILES),
-            in_=x.rearrange("(r p) k -> p r k", p=P),
-        )
+        x_sb = keep.tile([P, ROW_TILES, K], BF16)
         w2_sb = keep.tile([P, COL_TILES, NH], BF16)
-        nc.sync.dma_start(out=w2_sb[:], in_=W2.rearrange("(p t) h -> p t h", p=P))
+        w2_rows = W2.rearrange("(p t) h -> p t h", p=P)
         y_sb = keep.tile([P, ROW_TILES, N], BF16)
+        nc.sync.dma_start(out=w2_sb[:, 0:2], in_=w2_rows[:, 0:2])
+        nc.sync.dma_start(out=x_sb[:, 0], in_=x[0:P, :])
         nc.sync.dma_start(out=y_sb[:], in_=y.rearrange("(r p) n -> p r n", p=P))
+        nc.sync.dma_start(out=x_sb[:, 1], in_=x[P : 2 * P, :])
+        nc.sync.dma_start(out=w2_sb[:, 2:4], in_=w2_rows[:, 2:4])
         bias_lin_sb = keep.tile([P, COL_TILES], BF16)
         bias2_sb = keep.tile([P, COL_TILES], BF16)
         nc.scalar.dma_start(out=bias_lin_sb[:], in_=bias_lin.rearrange("(p t) -> p t", p=P))
@@ -65,13 +65,13 @@ def tile_advresnet_s_kernel(tc, x, y, beta, bias_lin, W1, W2, bias1, bias2, adv,
         table_warmer = keep.tile([P, 1], BF16)
         nc.scalar.copy(out=table_warmer[:], in_=ones[:])
 
-        busy_ps = psum.tile([P, P], F32)
+        acc = [psum.tile([P, N], F32, name="acc%d" % r) for r in range(ROW_TILES)]
 
         def keep_tensor_busy(count):
             for i in range(count):
-                nc.tensor.matmul(out=busy_ps[:], lhsT=ident[:], rhs=ident[:], start=True, stop=True)
+                nc.tensor.matmul(out=acc[1][:, 0:P], lhsT=ident[:], rhs=ident[:], start=True, stop=True)
 
-        keep_tensor_busy(2)
+        keep_tensor_busy(3)
 
         beta_abs = keep.tile([P, PASSES, PACK * N], BF16)
         beta_grouped = keep.tile([P, PASSES, N, PACK], BF16, align_bytes=64)
@@ -104,67 +104,6 @@ def tile_advresnet_s_kernel(tc, x, y, beta, bias_lin, W1, W2, bias1, bias2, adv,
             if g == 0:
                 keep_tensor_busy(2)
 
-        beta_codes = keep.tile([P, PASSES, N], U32, align_bytes=64)
-        beta_scales = keep.tile([P, PASSES, N], U8, align_bytes=64)
-        norm_sb = keep.tile([P, COL_TILES], F32)
-        for g in range(PASSES):
-            nc.vector.quantize_mx(
-                out=beta_codes[:, g].bitcast(FP8X4),
-                scales=beta_scales[:, g],
-                in_=beta_grouped[:, g].rearrange("p n t -> p (n t)"),
-            )
-            if g == 0:
-                nc.vector.tensor_reduce(out=norm_sb[:], in_=norm_ps[:], axis=AXIS.X, op=ALU.add)
-
-        x_words = x_sb[:].bitcast(F32).rearrange("p (r w) -> p r w", r=ROW_TILES)
-        x_grouped = keep.tile([P, PASSES * B * PACK], BF16, align_bytes=64)
-        x_grouped_words = x_grouped[:].bitcast(F32).rearrange("p (g row u) -> p g row u", g=PASSES, u=2)
-        x_codes = keep.tile([P, PASSES * B], U32, align_bytes=64)
-        x_scales = keep.tile([P, PASSES * B], U8, align_bytes=64)
-        for g in range(PASSES):
-            xt = psum.tile([P, 2, B], F32, name="xt%d" % g)
-            for u in range(2):
-                for r in range(ROW_TILES):
-                    first_word = 2 * g * P + u
-                    nc.tensor.transpose(
-                        xt[:, u, r * P : (r + 1) * P],
-                        x_words[:, r, first_word : (g + 1) * 2 * P : 2],
-                        ident[:],
-                    )
-            if g == 0:
-                nc.scalar.copy(out=x_grouped_words[:, g], in_=xt[:].rearrange("p u row -> p row u"))
-            else:
-                nc.vector.tensor_copy(out=x_grouped_words[:, g], in_=xt[:].rearrange("p u row -> p row u"))
-        keep_tensor_busy(2)
-        for g in range(PASSES):
-            nc.vector.quantize_mx(
-                out=x_codes[:, g * B : (g + 1) * B].bitcast(FP8X4),
-                scales=x_scales[:, g * B : (g + 1) * B],
-                in_=x_grouped[:, g * B * PACK : (g + 1) * B * PACK],
-            )
-
-        norm_rows = psum.tile([P, N], F32)
-        for j in range(COL_TILES):
-            nc.tensor.transpose(
-                norm_rows[:, j * P : (j + 1) * P],
-                norm_sb[:, j : j + 1].to_broadcast([P, P]),
-                ident[:],
-            )
-
-        acc = [psum.tile([P, N], F32, name="acc%d" % r) for r in range(ROW_TILES)]
-        for g in range(PASSES):
-            for r in range(ROW_TILES):
-                rows = slice(g * B + r * P, g * B + (r + 1) * P)
-                nc.tensor.matmul_mx(
-                    out=acc[r][:],
-                    lhsT=x_codes[:, rows].bitcast(FP8X4),
-                    lhsT_scale=x_scales[:, rows],
-                    rhs=beta_codes[:, g].bitcast(FP8X4),
-                    rhs_scale=beta_scales[:, g],
-                    start=(g == 0),
-                    stop=(g == PASSES - 1),
-                )
-
         bias_share = keep.tile([P, COL_TILES], F32)
         nc.gpsimd.tensor_tensor(out=bias_share[:], in0=bias_lin_sb[:], in1=bias2_sb[:], op=ALU.add)
         nc.gpsimd.tensor_scalar(
@@ -172,7 +111,8 @@ def tile_advresnet_s_kernel(tc, x, y, beta, bias_lin, W1, W2, bias1, bias2, adv,
         )
         summands = keep.tile([P, COL_TILES, NH], BF16)
         shift_sb = keep.tile([P, COL_TILES], F32)
-        for t in range(COL_TILES):
+
+        def sum_w2(t):
             nc.scalar.activation(
                 out=summands[:, t],
                 in_=w2_sb[:, t],
@@ -182,8 +122,52 @@ def tile_advresnet_s_kernel(tc, x, y, beta, bias_lin, W1, W2, bias1, bias2, adv,
                 accum_out=shift_sb[:, t : t + 1],
             )
 
+        x_grouped = keep.tile([P, ROW_TILES, PASSES * P * PACK], BF16, align_bytes=64)
+        x_codes = keep.tile([P, ROW_TILES, PASSES * P], U32, align_bytes=64)
+        x_scales = keep.tile([P, ROW_TILES, PASSES * P], U8, align_bytes=64)
+
+        def transpose_x(r):
+            words = x_sb[:, r].bitcast(F32)
+            xt = psum.tile([P, PASSES, 2, P], F32, name="xt%d" % r)
+            for g in range(PASSES):
+                for u in range(2):
+                    nc.tensor.transpose(xt[:, g, u, :], words[:, 2 * g * P + u : 2 * (g + 1) * P : 2], ident[:])
+            nc.scalar.copy(
+                out=x_grouped[:, r].bitcast(F32).rearrange("p (g row u) -> p g row u", g=PASSES, u=2),
+                in_=xt[:].rearrange("p g u row -> p g row u"),
+            )
+
+        def quantize_x(r):
+            nc.vector.quantize_mx(out=x_codes[:, r].bitcast(FP8X4), scales=x_scales[:, r], in_=x_grouped[:, r])
+
+        beta_codes = keep.tile([P, PASSES, N], U32, align_bytes=64)
+        beta_scales = keep.tile([P, PASSES, N], U8, align_bytes=64)
+
+        def quantize_beta(g):
+            nc.vector.quantize_mx(
+                out=beta_codes[:, g].bitcast(FP8X4),
+                scales=beta_scales[:, g],
+                in_=beta_grouped[:, g].rearrange("p n t -> p (n t)"),
+            )
+
+        def multiply(r):
+            for g in range(PASSES):
+                rows = slice(g * P, (g + 1) * P)
+                nc.tensor.matmul_mx(
+                    out=acc[r][:],
+                    lhsT=x_codes[:, r, rows].bitcast(FP8X4),
+                    lhsT_scale=x_scales[:, r, rows],
+                    rhs=beta_codes[:, g].bitcast(FP8X4),
+                    rhs_scale=beta_scales[:, g],
+                    start=(g == 0),
+                    stop=(g == PASSES - 1),
+                )
+
+        norm_sb = keep.tile([P, COL_TILES], F32)
+        norm_rows = psum.tile([P, N], F32)
         total = keep.tile([P, ROW_TILES, N], F32)
-        for r in range(ROW_TILES):
+
+        def start_total(r):
             nc.vector.scalar_tensor_tensor(
                 out=total[:, r],
                 in0=y_sb[:, r],
@@ -192,6 +176,28 @@ def tile_advresnet_s_kernel(tc, x, y, beta, bias_lin, W1, W2, bias1, bias2, adv,
                 op0=ALU.mult,
                 op1=ALU.mult,
             )
+
+        sum_w2(0)
+        quantize_beta(0)
+        transpose_x(0)
+        nc.vector.tensor_reduce(out=norm_sb[:], in_=norm_ps[:], axis=AXIS.X, op=ALU.add)
+        for j in range(COL_TILES):
+            nc.tensor.transpose(
+                norm_rows[:, j * P : (j + 1) * P],
+                norm_sb[:, j : j + 1].to_broadcast([P, P]),
+                ident[:],
+            )
+        quantize_beta(1)
+        keep_tensor_busy(1)
+        start_total(0)
+        quantize_x(0)
+        transpose_x(1)
+        start_total(1)
+        quantize_x(1)
+        for t in range(1, COL_TILES):
+            sum_w2(t)
+        for r in range(ROW_TILES):
+            multiply(r)
         for r in range(ROW_TILES):
             nc.vector.tensor_tensor(out=total[:, r], in0=total[:, r], in1=acc[r][:], op=ALU.add)
         shift_rows = psum.tile([P, COL_TILES, P], F32)

@@ -22,7 +22,7 @@ ROW_TILES = B // P
 COL_TILES = N // P
 EPSILON = 0.1
 
-VECTOR_COLS = 192
+VECTOR_COLS = 320
 
 FLOPS = 2 * B * K * N
 BYTES = 2 * (B * K + B * N + K * N + N * NH + 2 * N) + 4 * B * N
@@ -36,6 +36,17 @@ def tile_advresnet_s_kernel(tc, x, y, beta, bias_lin, W1, W2, bias1, bias2, adv,
         psum = ctx.enter_context(tc.psum_pool(name="psum", bufs=1))
         ctx.enter_context(tc.manual_schedule())
 
+        ones = keep.tile([P, 1], BF16)
+        nc.vector.memset(ones[:], 1.0)
+        bias_rows = keep.tile([P, P], BF16)
+        nc.vector.memset(bias_rows[:], 0.0)
+        table_warmer = keep.tile([P, 1], BF16)
+        nc.scalar.copy(out=table_warmer[:], in_=ones[:])
+        ident = keep.tile([P, P], F32)
+        make_identity(nc, ident[:])
+        ident_bf = keep.tile([P, P], BF16)
+        nc.gpsimd.tensor_copy(out=ident_bf[:], in_=ident[:])
+
         beta_sb = keep.tile([P, PASSES, PACK, N], BF16)
         for g in range(PASSES):
             for u in range(2):
@@ -44,104 +55,82 @@ def tile_advresnet_s_kernel(tc, x, y, beta, bias_lin, W1, W2, bias1, bias2, adv,
                     out=beta_sb[:, g, 2 * u : 2 * u + 2, :],
                     in_=rows_of_pass[:, 2 * u : 2 * u + 2, :],
                 )
+            if g == 0:
+                for part, bias in enumerate((bias_lin, bias2)):
+                    nc.sync.dma_start(
+                        out=bias_rows[part * COL_TILES : (part + 1) * COL_TILES, :],
+                        in_=bias.rearrange("(j p) -> j p", p=P),
+                    )
         x_sb = keep.tile([P, ROW_TILES, K], BF16)
         w2_sb = keep.tile([P, COL_TILES, NH], BF16)
-        w2_rows = W2.rearrange("(p t) h -> p t h", p=P)
+        for r in range(ROW_TILES):
+            nc.sync.dma_start(out=x_sb[:, r], in_=x[r * P : (r + 1) * P, :])
+        nc.sync.dma_start(out=w2_sb[:], in_=W2.rearrange("(j p) h -> p j h", p=P))
         y_sb = keep.tile([P, ROW_TILES, N], BF16)
-        nc.sync.dma_start(out=w2_sb[:, 0:2], in_=w2_rows[:, 0:2])
-        nc.sync.dma_start(out=x_sb[:, 0], in_=x[0:P, :])
         nc.sync.dma_start(out=y_sb[:], in_=y.rearrange("(r p) n -> p r n", p=P))
-        nc.sync.dma_start(out=x_sb[:, 1], in_=x[P : 2 * P, :])
-        nc.sync.dma_start(out=w2_sb[:, 2:4], in_=w2_rows[:, 2:4])
-        bias_lin_sb = keep.tile([P, COL_TILES], BF16)
-        bias2_sb = keep.tile([P, COL_TILES], BF16)
-        nc.scalar.dma_start(out=bias_lin_sb[:], in_=bias_lin.rearrange("(p t) -> p t", p=P))
-        nc.scalar.dma_start(out=bias2_sb[:], in_=bias2.rearrange("(p t) -> p t", p=P))
 
-        ident = keep.tile([P, P], F32)
-        make_identity(nc, ident[:])
-        ones = keep.tile([P, 1], BF16)
-        nc.vector.memset(ones[:], 1.0)
-        table_warmer = keep.tile([P, 1], BF16)
-        nc.scalar.copy(out=table_warmer[:], in_=ones[:])
-
-        acc = [psum.tile([P, N], F32, name="acc%d" % r) for r in range(ROW_TILES)]
+        acc = [psum.tile([P, N], F32, name="acc%d" % j) for j in range(COL_TILES)]
 
         def keep_tensor_busy(count):
             for i in range(count):
-                nc.tensor.matmul(out=acc[1][:, 0:P], lhsT=ident[:], rhs=ident[:], start=True, stop=True)
+                nc.tensor.matmul(out=acc[3][:, 0:P], lhsT=ident[:], rhs=ident[:], start=True, stop=True)
 
         keep_tensor_busy(3)
 
         beta_abs = keep.tile([P, PASSES, PACK * N], BF16)
         beta_grouped = keep.tile([P, PASSES, N, PACK], BF16, align_bytes=64)
-        norm_ps = psum.tile([P, COL_TILES, PASSES], F32)
-        for g in range(PASSES):
-            for u in range(2):
-                pair = slice(2 * u * N, (2 * u + 2) * N)
-                nc.vector.tensor_scalar(
-                    out=beta_abs[:, g, pair].bitcast(I32),
-                    in0=beta_sb[:, g].rearrange("p t n -> p (t n)")[:, pair].bitcast(I32),
-                    scalar1=0x7FFF7FFF,
-                    scalar2=None,
-                    op0=ALU.bitwise_and,
-                )
+        sums_bank = psum.tile([P, N], F32)
+        sums = sums_bank[:, 0 : COL_TILES * (PASSES + 1)].rearrange("p (j part) -> p j part", part=PASSES + 1)
+
+        def clear_signs(g, u):
+            pair = slice(2 * u * N, (2 * u + 2) * N)
+            nc.vector.tensor_scalar(
+                out=beta_abs[:, g, pair].bitcast(I32),
+                in0=beta_sb[:, g].rearrange("p t n -> p (t n)")[:, pair].bitcast(I32),
+                scalar1=0x7FFF7FFF,
+                scalar2=None,
+                op0=ALU.bitwise_and,
+            )
+
+        def regroup(g):
             src = beta_sb[:, g].rearrange("p t (c i) -> p c t i", i=4)
             dst = beta_grouped[:, g].rearrange("p (c i) t -> p c t i", i=4)
             cut = VECTOR_COLS // 4
             nc.vector.tensor_copy(out=dst[:, :cut], in_=src[:, :cut])
             nc.scalar.copy(out=dst[:, cut:], in_=src[:, cut:])
+
+        def sum_columns(g):
             for j in range(COL_TILES):
                 for t in range(PACK):
                     first = t * N + j * P
                     nc.tensor.matmul(
-                        out=norm_ps[:, j, g : g + 1],
+                        out=sums[:, j, g : g + 1],
                         lhsT=beta_abs[:, g, first : first + P],
                         rhs=ones[:],
                         start=(t == 0),
                         stop=(t == PACK - 1),
                     )
-            if g == 0:
-                keep_tensor_busy(2)
 
-        bias_share = keep.tile([P, COL_TILES], F32)
-        nc.gpsimd.tensor_tensor(out=bias_share[:], in0=bias_lin_sb[:], in1=bias2_sb[:], op=ALU.add)
-        nc.gpsimd.tensor_scalar(
-            out=bias_share[:], in0=bias_share[:], scalar1=1.0 / NH, scalar2=0.0, op0=ALU.mult, op1=ALU.add
-        )
-        summands = keep.tile([P, COL_TILES, NH], BF16)
-        shift_sb = keep.tile([P, COL_TILES], F32)
-
-        def sum_w2(t):
-            nc.scalar.activation(
-                out=summands[:, t],
-                in_=w2_sb[:, t],
-                func=ACT.Identity,
-                scale=float(NH),
-                bias=bias_share[:, t : t + 1],
-                accum_out=shift_sb[:, t : t + 1],
-            )
-
-        x_grouped = keep.tile([P, ROW_TILES, PASSES * P * PACK], BF16, align_bytes=64)
-        x_codes = keep.tile([P, ROW_TILES, PASSES * P], U32, align_bytes=64)
-        x_scales = keep.tile([P, ROW_TILES, PASSES * P], U8, align_bytes=64)
+        x_grouped = keep.tile([P, PASSES, B, PACK], BF16, align_bytes=64)
+        x_grouped_words = x_grouped[:].rearrange("p g row t -> p (g row t)").bitcast(F32)
+        x_grouped_words = x_grouped_words.rearrange("p (g row u) -> p g row u", g=PASSES, u=2)
 
         def transpose_x(r):
             words = x_sb[:, r].bitcast(F32)
-            xt = psum.tile([P, PASSES, 2, P], F32, name="xt%d" % r)
+            xt_bank = psum.tile([P, N], F32, name="xt%d" % r)
+            xt = xt_bank[:].rearrange("p (g u row) -> p g u row", g=PASSES, u=2)
             for g in range(PASSES):
                 for u in range(2):
                     nc.tensor.transpose(xt[:, g, u, :], words[:, 2 * g * P + u : 2 * (g + 1) * P : 2], ident[:])
             nc.scalar.copy(
-                out=x_grouped[:, r].bitcast(F32).rearrange("p (g row u) -> p g row u", g=PASSES, u=2),
-                in_=xt[:].rearrange("p g u row -> p g row u"),
+                out=x_grouped_words[:, :, r * P : (r + 1) * P],
+                in_=xt.rearrange("p g u row -> p g row u"),
             )
-
-        def quantize_x(r):
-            nc.vector.quantize_mx(out=x_codes[:, r].bitcast(FP8X4), scales=x_scales[:, r], in_=x_grouped[:, r])
 
         beta_codes = keep.tile([P, PASSES, N], U32, align_bytes=64)
         beta_scales = keep.tile([P, PASSES, N], U8, align_bytes=64)
+        x_codes = keep.tile([P, PASSES * B], U32, align_bytes=64)
+        x_scales = keep.tile([P, PASSES * B], U8, align_bytes=64)
 
         def quantize_beta(g):
             nc.vector.quantize_mx(
@@ -150,66 +139,128 @@ def tile_advresnet_s_kernel(tc, x, y, beta, bias_lin, W1, W2, bias1, bias2, adv,
                 in_=beta_grouped[:, g].rearrange("p n t -> p (n t)"),
             )
 
-        def multiply(r):
-            for g in range(PASSES):
-                rows = slice(g * P, (g + 1) * P)
+        def keep_tensor_busy_mx(count):
+            for i in range(count):
                 nc.tensor.matmul_mx(
-                    out=acc[r][:],
-                    lhsT=x_codes[:, r, rows].bitcast(FP8X4),
-                    lhsT_scale=x_scales[:, r, rows],
-                    rhs=beta_codes[:, g].bitcast(FP8X4),
-                    rhs_scale=beta_scales[:, g],
+                    out=acc[3][:],
+                    lhsT=beta_codes[:, 0, 0:P].bitcast(FP8X4),
+                    lhsT_scale=beta_scales[:, 0, 0:P],
+                    rhs=beta_codes[:, 0].bitcast(FP8X4),
+                    rhs_scale=beta_scales[:, 0],
+                    start=True,
+                    stop=True,
+                )
+
+        bias_share = keep.tile([P, COL_TILES], F32)
+        summands = keep.tile([P, COL_TILES, NH], BF16)
+        shift = keep.tile([P, COL_TILES], F32)
+        row_sum = keep.tile([P, 1], F32)
+
+        def sum_biases():
+            for part in range(2):
+                nc.tensor.matmul(
+                    out=sums[:, :, PASSES],
+                    lhsT=bias_rows[:],
+                    rhs=ident_bf[:, part * COL_TILES : (part + 1) * COL_TILES],
+                    start=(part == 0),
+                    stop=(part == 1),
+                )
+            nc.vector.tensor_scalar(
+                out=bias_share[:], in0=sums[:, :, PASSES], scalar1=1.0 / NH, scalar2=None, op0=ALU.mult
+            )
+
+        def sum_w2_on_vector(j):
+            nc.vector.tensor_scalar(
+                out=summands[:, j],
+                in0=w2_sb[:, j],
+                scalar1=float(NH),
+                scalar2=None,
+                op0=ALU.mult,
+                op1=ALU.add,
+                accum_out=row_sum[:],
+            )
+            nc.vector.tensor_tensor(
+                out=shift[:, j : j + 1], in0=row_sum[:], in1=sums[:, j, PASSES : PASSES + 1], op=ALU.add
+            )
+
+        def sum_w2(j):
+            nc.scalar.activation(
+                out=summands[:, j],
+                in_=w2_sb[:, j],
+                func=ACT.Identity,
+                scale=float(NH),
+                bias=bias_share[:, j : j + 1],
+                accum_out=shift[:, j : j + 1],
+            )
+
+        clear_signs(0, 0)
+        clear_signs(0, 1)
+        regroup(0)
+        sum_columns(0)
+        keep_tensor_busy(2)
+        clear_signs(1, 0)
+        clear_signs(1, 1)
+        regroup(1)
+        sum_biases()
+        transpose_x(0)
+        transpose_x(1)
+        sum_columns(1)
+        quantize_beta(0)
+        quantize_beta(1)
+        keep_tensor_busy_mx(2)
+        norm = keep.tile([P, COL_TILES], F32)
+        nc.vector.tensor_reduce(out=norm[:], in_=sums[:, :, 0:PASSES], axis=AXIS.X, op=ALU.add)
+        norm_rows = psum.tile([P, N], F32)
+        for j in range(COL_TILES):
+            nc.tensor.transpose(
+                norm_rows[:, j * P : (j + 1) * P],
+                norm[:, j : j + 1].to_broadcast([P, P]),
+                ident[:],
+            )
+        nc.vector.quantize_mx(
+            out=x_codes[:].bitcast(FP8X4), scales=x_scales[:], in_=x_grouped[:].rearrange("p g row t -> p (g row t)")
+        )
+        keep_tensor_busy_mx(1)
+        for j in range(3):
+            sum_w2(j)
+        sum_w2_on_vector(3)
+
+        for j in range(COL_TILES):
+            for g in range(PASSES):
+                cols = slice(j * P, (j + 1) * P)
+                rows = slice(g * B, (g + 1) * B)
+                nc.tensor.matmul_mx(
+                    out=acc[j][:, 0:B],
+                    lhsT=beta_codes[:, g, cols].bitcast(FP8X4),
+                    lhsT_scale=beta_scales[:, g, cols],
+                    rhs=x_codes[:, rows].bitcast(FP8X4),
+                    rhs_scale=x_scales[:, rows],
                     start=(g == 0),
                     stop=(g == PASSES - 1),
                 )
 
-        norm_sb = keep.tile([P, COL_TILES], F32)
-        norm_rows = psum.tile([P, N], F32)
         total = keep.tile([P, ROW_TILES, N], F32)
-
-        def start_total(r):
+        for half in range(2):
+            cols = slice(half * N // 2, (half + 1) * N // 2)
             nc.vector.scalar_tensor_tensor(
-                out=total[:, r],
-                in0=y_sb[:, r],
+                out=total[:, :, cols],
+                in0=y_sb[:, :, cols],
                 scalar=-EPSILON,
-                in1=norm_rows[:],
+                in1=norm_rows[:, cols].unsqueeze(1).to_broadcast([P, ROW_TILES, N // 2]),
                 op0=ALU.mult,
                 op1=ALU.mult,
             )
 
-        sum_w2(0)
-        quantize_beta(0)
-        transpose_x(0)
-        nc.vector.tensor_reduce(out=norm_sb[:], in_=norm_ps[:], axis=AXIS.X, op=ALU.add)
+        product = keep.tile([P, COL_TILES, B], F32)
         for j in range(COL_TILES):
-            nc.tensor.transpose(
-                norm_rows[:, j * P : (j + 1) * P],
-                norm_sb[:, j : j + 1].to_broadcast([P, P]),
-                ident[:],
-            )
-        quantize_beta(1)
-        keep_tensor_busy(1)
-        start_total(0)
-        quantize_x(0)
-        transpose_x(1)
-        start_total(1)
-        quantize_x(1)
-        for t in range(1, COL_TILES):
-            sum_w2(t)
-        for r in range(ROW_TILES):
-            multiply(r)
-        for r in range(ROW_TILES):
-            nc.vector.tensor_tensor(out=total[:, r], in0=total[:, r], in1=acc[r][:], op=ALU.add)
-        shift_rows = psum.tile([P, COL_TILES, P], F32)
-        for t in range(COL_TILES):
-            nc.tensor.transpose(
-                shift_rows[:, t, :],
-                shift_sb[:, t : t + 1].to_broadcast([P, P]),
-                ident[:],
-            )
-        for r in range(ROW_TILES):
-            total_qt = total[:, r].rearrange("p (q t) -> p q t", t=COL_TILES)
+            nc.scalar.activation(out=product[:, j], in_=acc[j][:, 0:B], func=ACT.Identity, bias=shift[:, j : j + 1])
+        for j, bank in enumerate(("xt0", "xt1", "sums_bank", "acc0")):
+            cols = slice(j * P, (j + 1) * P)
+            bank_tile = psum.tile([P, N], F32, name=bank)
+            product_rows = bank_tile[:, 0 : ROW_TILES * P].rearrange("p (r c) -> p r c", r=ROW_TILES)
+            for r in range(ROW_TILES):
+                nc.tensor.transpose(product_rows[:, r], product[:, j, r * P : (r + 1) * P], ident[:])
             nc.vector.tensor_tensor(
-                out=total_qt, in0=total_qt, in1=shift_rows[:].rearrange("p t q -> p q t"), op=ALU.add
+                out=total[:, :, cols], in0=total[:, :, cols], in1=product_rows, op=ALU.add
             )
-            nc.sync.dma_start(out=out[r * P : (r + 1) * P, :], in_=total[:, r])
+            nc.sync.dma_start(out=out.rearrange("(r p) n -> p r n", p=P)[:, :, cols], in_=total[:, :, cols])

@@ -23,6 +23,7 @@ COL_TILES = N // P
 EPSILON = 0.1
 
 VECTOR_COLS = 320
+SCALAR_SUMS = 2
 
 FLOPS = 2 * B * K * N
 BYTES = 2 * (B * K + B * N + K * N + N * NH + 2 * N) + 4 * B * N
@@ -154,7 +155,7 @@ def tile_advresnet_s_kernel(tc, x, y, beta, bias_lin, W1, W2, bias1, bias2, adv,
         bias_share = keep.tile([P, COL_TILES], F32)
         summands = keep.tile([P, COL_TILES, NH], BF16)
         shift = keep.tile([P, COL_TILES], F32)
-        row_sum = keep.tile([P, 1], F32)
+        row_sums = keep.tile([P, COL_TILES], F32)
 
         def sum_biases():
             for part in range(2):
@@ -177,10 +178,12 @@ def tile_advresnet_s_kernel(tc, x, y, beta, bias_lin, W1, W2, bias1, bias2, adv,
                 scalar2=None,
                 op0=ALU.mult,
                 op1=ALU.add,
-                accum_out=row_sum[:],
+                accum_out=row_sums[:, j : j + 1],
             )
+
+        def add_biases_on_vector(first):
             nc.vector.tensor_tensor(
-                out=shift[:, j : j + 1], in0=row_sum[:], in1=sums[:, j, PASSES : PASSES + 1], op=ALU.add
+                out=shift[:, first:], in0=row_sums[:, first:], in1=sums[:, first:, PASSES], op=ALU.add
             )
 
         def sum_w2(j):
@@ -197,11 +200,11 @@ def tile_advresnet_s_kernel(tc, x, y, beta, bias_lin, W1, W2, bias1, bias2, adv,
         clear_signs(0, 1)
         regroup(0)
         sum_columns(0)
-        keep_tensor_busy(2)
         clear_signs(1, 0)
         clear_signs(1, 1)
         regroup(1)
         sum_biases()
+        keep_tensor_busy(1)
         transpose_x(0)
         transpose_x(1)
         sum_columns(1)
@@ -221,9 +224,11 @@ def tile_advresnet_s_kernel(tc, x, y, beta, bias_lin, W1, W2, bias1, bias2, adv,
             out=x_codes[:].bitcast(FP8X4), scales=x_scales[:], in_=x_grouped[:].rearrange("p g row t -> p (g row t)")
         )
         keep_tensor_busy_mx(1)
-        for j in range(3):
-            sum_w2(j)
-        sum_w2_on_vector(3)
+        for j in range(COL_TILES):
+            if j < SCALAR_SUMS:
+                sum_w2(j)
+            else:
+                sum_w2_on_vector(j)
 
         for j in range(COL_TILES):
             for g in range(PASSES):
@@ -250,6 +255,8 @@ def tile_advresnet_s_kernel(tc, x, y, beta, bias_lin, W1, W2, bias1, bias2, adv,
                 op0=ALU.mult,
                 op1=ALU.mult,
             )
+            if half == 0:
+                add_biases_on_vector(SCALAR_SUMS)
 
         product = keep.tile([P, COL_TILES, B], F32)
         for j in range(COL_TILES):

@@ -100,7 +100,7 @@ def tile_advresnet_s_kernel(tc, x, y, beta, bias_lin, W1, W2, bias1, bias2, adv,
             nc.vector.tensor_copy(out=dst[:, :cut], in_=src[:, :cut])
             nc.scalar.copy(out=dst[:, cut:], in_=src[:, cut:])
 
-        def sum_columns(g):
+        def sum_columns(g, busy_after_first=0):
             for j in range(COL_TILES):
                 for t in range(PACK):
                     first = t * N + j * P
@@ -111,6 +111,8 @@ def tile_advresnet_s_kernel(tc, x, y, beta, bias_lin, W1, W2, bias1, bias2, adv,
                         start=(t == 0),
                         stop=(t == PACK - 1),
                     )
+                    if j == 0 and t == 1:
+                        keep_tensor_busy(busy_after_first)
 
         x_grouped = keep.tile([P, PASSES, B, PACK], BF16, align_bytes=64)
         x_grouped_words = x_grouped[:].rearrange("p g row t -> p (g row t)").bitcast(F32)
@@ -199,12 +201,12 @@ def tile_advresnet_s_kernel(tc, x, y, beta, bias_lin, W1, W2, bias1, bias2, adv,
         clear_signs(0, 0)
         clear_signs(0, 1)
         regroup(0)
-        sum_columns(0)
+        sum_columns(0, busy_after_first=1)
+        keep_tensor_busy(2)
         clear_signs(1, 0)
         clear_signs(1, 1)
         regroup(1)
         sum_biases()
-        keep_tensor_busy(1)
         transpose_x(0)
         transpose_x(1)
         sum_columns(1)

@@ -159,7 +159,7 @@ def tile_advresnet_s_kernel(tc, x, y, beta, bias_lin, W1, W2, bias1, bias2, adv,
         shift = keep.tile([P, COL_TILES], F32)
         row_sums = keep.tile([P, COL_TILES], F32)
 
-        def sum_biases():
+        def sum_biases_on_tensor():
             for part in range(2):
                 nc.tensor.matmul(
                     out=sums[:, :, PASSES],
@@ -168,6 +168,8 @@ def tile_advresnet_s_kernel(tc, x, y, beta, bias_lin, W1, W2, bias1, bias2, adv,
                     start=(part == 0),
                     stop=(part == 1),
                 )
+
+        def share_biases():
             nc.vector.tensor_scalar(
                 out=bias_share[:], in0=sums[:, :, PASSES], scalar1=1.0 / NH, scalar2=None, op0=ALU.mult
             )
@@ -206,12 +208,13 @@ def tile_advresnet_s_kernel(tc, x, y, beta, bias_lin, W1, W2, bias1, bias2, adv,
         clear_signs(1, 0)
         clear_signs(1, 1)
         regroup(1)
-        sum_biases()
         transpose_x(0)
         transpose_x(1)
+        sum_biases_on_tensor()
         sum_columns(1)
         quantize_beta(0)
         quantize_beta(1)
+        share_biases()
         keep_tensor_busy_mx(2)
         norm = keep.tile([P, COL_TILES], F32)
         nc.vector.tensor_reduce(out=norm[:], in_=sums[:, :, 0:PASSES], axis=AXIS.X, op=ALU.add)

@@ -50,12 +50,13 @@ def tile_advresnet_s_kernel(tc, x, y, beta, bias_lin, W1, W2, bias1, bias2, adv,
 
         beta_sb = keep.tile([P, PASSES, PACK, N], BF16)
         for g in range(PASSES):
-            for u in range(2):
-                rows_of_pass = beta[g * K_PASS : (g + 1) * K_PASS, :].rearrange("(p t) n -> p t n", t=PACK)
-                nc.sync.dma_start(
-                    out=beta_sb[:, g, 2 * u : 2 * u + 2, :],
-                    in_=rows_of_pass[:, 2 * u : 2 * u + 2, :],
-                )
+            rows_of_pass = beta[g * K_PASS : (g + 1) * K_PASS, :].rearrange("(p t) n -> p t n", t=PACK)
+            if g == 0:
+                for u in range(2):
+                    pair = slice(2 * u, 2 * u + 2)
+                    nc.sync.dma_start(out=beta_sb[:, g, pair], in_=rows_of_pass[:, pair])
+            else:
+                nc.sync.dma_start(out=beta_sb[:, g], in_=rows_of_pass)
             if g == 0:
                 for part, bias in enumerate((bias_lin, bias2)):
                     nc.sync.dma_start(
@@ -63,12 +64,16 @@ def tile_advresnet_s_kernel(tc, x, y, beta, bias_lin, W1, W2, bias1, bias2, adv,
                         in_=bias.rearrange("(j p) -> j p", p=P),
                     )
         x_sb = keep.tile([P, ROW_TILES, K], BF16)
+        x_rows = x.rearrange("(p r) k -> p r k", p=P)
         w2_sb = keep.tile([P, COL_TILES, NH], BF16)
         for r in range(ROW_TILES):
-            nc.sync.dma_start(out=x_sb[:, r], in_=x[r * P : (r + 1) * P, :])
-        nc.sync.dma_start(out=w2_sb[:], in_=W2.rearrange("(j p) h -> p j h", p=P))
+            nc.sync.dma_start(out=x_sb[:, r], in_=x_rows[:, r])
+        w2_rows = W2.rearrange("(j p) h -> p j h", p=P)
+        for half in range(2):
+            pair = slice(2 * half, 2 * half + 2)
+            nc.sync.dma_start(out=w2_sb[:, pair], in_=w2_rows[:, pair])
         y_sb = keep.tile([P, ROW_TILES, N], BF16)
-        nc.sync.dma_start(out=y_sb[:], in_=y.rearrange("(r p) n -> p r n", p=P))
+        nc.sync.dma_start(out=y_sb[:], in_=y.rearrange("(p r) n -> p r n", p=P))
 
         acc = [psum.tile([P, N], F32, name="acc%d" % j) for j in range(COL_TILES)]
 
@@ -275,4 +280,4 @@ def tile_advresnet_s_kernel(tc, x, y, beta, bias_lin, W1, W2, bias1, bias2, adv,
             nc.vector.tensor_tensor(
                 out=total[:, :, cols], in0=total[:, :, cols], in1=product_rows, op=ALU.add
             )
-            nc.sync.dma_start(out=out.rearrange("(r p) n -> p r n", p=P)[:, :, cols], in_=total[:, :, cols])
+            nc.sync.dma_start(out=out.rearrange("(p r) n -> p r n", p=P)[:, :, cols], in_=total[:, :, cols])

@@ -75,7 +75,13 @@ def tile_advresnet_s_kernel(tc, x, y, beta, bias_lin, W1, W2, bias1, bias2, adv,
         y_sb = keep.tile([P, ROW_TILES, N], BF16)
         nc.sync.dma_start(out=y_sb[:], in_=y.rearrange("(p r) n -> p r n", p=P))
 
-        acc = [psum.tile([P, N], F32, name="acc%d" % j) for j in range(COL_TILES)]
+        acc = {}
+
+        def open_acc(j):
+            acc[j] = psum.tile([P, N], F32, name="acc%d" % j)
+
+        for j in (1, 2, 3):
+            open_acc(j)
 
         def keep_tensor_busy(count):
             for i in range(count):
@@ -88,8 +94,8 @@ def tile_advresnet_s_kernel(tc, x, y, beta, bias_lin, W1, W2, bias1, bias2, adv,
         sums_bank = psum.tile([P, N], F32)
         sums = sums_bank[:, 0 : COL_TILES * (PASSES + 1)].rearrange("p (j part) -> p j part", part=PASSES + 1)
 
-        def clear_signs(g, u):
-            pair = slice(2 * u * N, (2 * u + 2) * N)
+        def clear_signs(g, first=0, last=PACK):
+            pair = slice(first * N, last * N)
             nc.vector.tensor_scalar(
                 out=beta_abs[:, g, pair].bitcast(I32),
                 in0=beta_sb[:, g].rearrange("p t n -> p (t n)")[:, pair].bitcast(I32),
@@ -125,15 +131,14 @@ def tile_advresnet_s_kernel(tc, x, y, beta, bias_lin, W1, W2, bias1, bias2, adv,
 
         def transpose_x(r):
             words = x_sb[:, r].bitcast(F32)
-            xt_bank = psum.tile([P, N], F32, name="xt%d" % r)
-            xt = xt_bank[:].rearrange("p (g u row) -> p g u row", g=PASSES, u=2)
             for g in range(PASSES):
+                xt_bank = psum.tile([P, N], F32, name=(("xt0", "xt1"), ("norm_rows", "acc0"))[r][g])
+                xt = xt_bank[:, 0 : 2 * P].rearrange("p (u row) -> p u row", u=2)
                 for u in range(2):
-                    nc.tensor.transpose(xt[:, g, u, :], words[:, 2 * g * P + u : 2 * (g + 1) * P : 2], ident[:])
-            nc.scalar.copy(
-                out=x_grouped_words[:, :, r * P : (r + 1) * P],
-                in_=xt.rearrange("p g u row -> p g row u"),
-            )
+                    nc.tensor.transpose(xt[:, u, :], words[:, 2 * g * P + u : 2 * (g + 1) * P : 2], ident[:])
+                nc.scalar.copy(
+                    out=x_grouped_words[:, g, r * P : (r + 1) * P], in_=xt.rearrange("p u row -> p row u")
+                )
 
         beta_codes = keep.tile([P, PASSES, N], U32, align_bytes=64)
         beta_scales = keep.tile([P, PASSES, N], U8, align_bytes=64)
@@ -159,10 +164,10 @@ def tile_advresnet_s_kernel(tc, x, y, beta, bias_lin, W1, W2, bias1, bias2, adv,
                     stop=True,
                 )
 
-        bias_share = keep.tile([P, COL_TILES], F32)
+        bias_share = keep.tile([P, SCALAR_SUMS], F32)
+        bias_sum = keep.tile([P, COL_TILES - SCALAR_SUMS], F32)
         summands = keep.tile([P, COL_TILES, NH], BF16)
         shift = keep.tile([P, COL_TILES], F32)
-        row_sums = keep.tile([P, COL_TILES], F32)
 
         def sum_biases_on_tensor():
             for part in range(2):
@@ -174,25 +179,21 @@ def tile_advresnet_s_kernel(tc, x, y, beta, bias_lin, W1, W2, bias1, bias2, adv,
                     stop=(part == 1),
                 )
 
-        def share_biases():
-            nc.vector.tensor_scalar(
-                out=bias_share[:], in0=sums[:, :, PASSES], scalar1=1.0 / NH, scalar2=None, op0=ALU.mult
+        def copy_biases_on_scalar():
+            nc.scalar.activation(
+                out=bias_share[:], in_=sums[:, 0:SCALAR_SUMS, PASSES], func=ACT.Copy, scale=1.0 / NH
             )
+            nc.scalar.copy(out=bias_sum[:], in_=sums[:, SCALAR_SUMS:, PASSES])
 
         def sum_w2_on_vector(j):
             nc.vector.tensor_scalar(
                 out=summands[:, j],
                 in0=w2_sb[:, j],
                 scalar1=float(NH),
-                scalar2=None,
+                scalar2=bias_sum[:, j - SCALAR_SUMS : j - SCALAR_SUMS + 1],
                 op0=ALU.mult,
                 op1=ALU.add,
-                accum_out=row_sums[:, j : j + 1],
-            )
-
-        def add_biases_on_vector(first):
-            nc.vector.tensor_tensor(
-                out=shift[:, first:], in0=row_sums[:, first:], in1=sums[:, first:, PASSES], op=ALU.add
+                accum_out=shift[:, j : j + 1],
             )
 
         def sum_w2(j):
@@ -205,21 +206,20 @@ def tile_advresnet_s_kernel(tc, x, y, beta, bias_lin, W1, W2, bias1, bias2, adv,
                 accum_out=shift[:, j : j + 1],
             )
 
-        clear_signs(0, 0)
-        clear_signs(0, 1)
+        clear_signs(0, 0, 2)
+        clear_signs(0, 2, 4)
         regroup(0)
         sum_columns(0, busy_after_first=1)
+        sum_biases_on_tensor()
         keep_tensor_busy(2)
-        clear_signs(1, 0)
-        clear_signs(1, 1)
+        clear_signs(1)
         regroup(1)
+        copy_biases_on_scalar()
         transpose_x(0)
         transpose_x(1)
-        sum_biases_on_tensor()
         sum_columns(1)
         quantize_beta(0)
         quantize_beta(1)
-        share_biases()
         keep_tensor_busy_mx(2)
         norm = keep.tile([P, COL_TILES], F32)
         nc.vector.tensor_reduce(out=norm[:], in_=sums[:, :, 0:PASSES], axis=AXIS.X, op=ALU.add)
@@ -233,13 +233,13 @@ def tile_advresnet_s_kernel(tc, x, y, beta, bias_lin, W1, W2, bias1, bias2, adv,
         nc.vector.quantize_mx(
             out=x_codes[:].bitcast(FP8X4), scales=x_scales[:], in_=x_grouped[:].rearrange("p g row t -> p (g row t)")
         )
-        keep_tensor_busy_mx(1)
         for j in range(COL_TILES):
             if j < SCALAR_SUMS:
                 sum_w2(j)
             else:
                 sum_w2_on_vector(j)
 
+        open_acc(0)
         for j in range(COL_TILES):
             for g in range(PASSES):
                 cols = slice(j * P, (j + 1) * P)
@@ -265,8 +265,6 @@ def tile_advresnet_s_kernel(tc, x, y, beta, bias_lin, W1, W2, bias1, bias2, adv,
                 op0=ALU.mult,
                 op1=ALU.mult,
             )
-            if half == 0:
-                add_biases_on_vector(SCALAR_SUMS)
 
         product = keep.tile([P, COL_TILES, B], F32)
         for j in range(COL_TILES):

from contextlib import ExitStack

import concourse.mybir as mybir
from concourse.masks import make_identity

F32 = mybir.dt.float32
BF16 = mybir.dt.bfloat16
I32 = mybir.dt.int32
U32 = mybir.dt.uint32
U8 = mybir.dt.uint8
FP8X4 = mybir.dt.float8_e4m3fn_x4
ALU = mybir.AluOpType
ACT = mybir.ActivationFunctionType
AXIS = mybir.AxisListType

P = 128
PACK = 4
K_PASS = P * PACK
B, K, N, NH = 256, 1024, 512, 512
PASSES = K // K_PASS
ROW_TILES = B // P
COL_TILES = N // P
EPSILON = 0.1

VECTOR_COLS = 320
SCALAR_SUMS = 2

FLOPS = 2 * B * K * N
BYTES = 2 * (B * K + B * N + K * N + N * NH + 2 * N) + 4 * B * N


def tile_advresnet_s_kernel(tc, x, y, beta, bias_lin, W1, W2, bias1, bias2, adv, out):
    assert adv == 1
    nc = tc.nc
    with ExitStack() as ctx:
        keep = ctx.enter_context(tc.tile_pool(name="keep", bufs=1))
        psum = ctx.enter_context(tc.psum_pool(name="psum", bufs=1))
        ctx.enter_context(tc.manual_schedule())

        ones = keep.tile([P, 1], BF16)
        nc.vector.memset(ones[:], 1.0)
        bias_rows = keep.tile([P, P], BF16)
        nc.vector.memset(bias_rows[:], 0.0)
        table_warmer = keep.tile([P, 1], BF16)
        nc.scalar.copy(out=table_warmer[:], in_=ones[:])
        ident = keep.tile([P, P], F32)
        make_identity(nc, ident[:])
        ident_bf = keep.tile([P, P], BF16)
        nc.gpsimd.tensor_copy(out=ident_bf[:], in_=ident[:])

        beta_sb = keep.tile([P, PASSES, PACK, N], BF16)
        for g in range(PASSES):
            rows_of_pass = beta[g * K_PASS : (g + 1) * K_PASS, :].rearrange("(p t) n -> p t n", t=PACK)
            if g == 0:
                for u in range(2):
                    pair = slice(2 * u, 2 * u + 2)
                    nc.sync.dma_start(out=beta_sb[:, g, pair], in_=rows_of_pass[:, pair])
            else:
                nc.sync.dma_start(out=beta_sb[:, g], in_=rows_of_pass)
            if g == 0:
                for part, bias in enumerate((bias_lin, bias2)):
                    nc.sync.dma_start(
                        out=bias_rows[part * COL_TILES : (part + 1) * COL_TILES, :],
                        in_=bias.rearrange("(j p) -> j p", p=P),
                    )
        x_sb = keep.tile([P, ROW_TILES, K], BF16)
        x_rows = x.rearrange("(p r) k -> p r k", p=P)
        w2_sb = keep.tile([P, COL_TILES, NH], BF16)
        for r in range(ROW_TILES):
            nc.sync.dma_start(out=x_sb[:, r], in_=x_rows[:, r])
        w2_rows = W2.rearrange("(j p) h -> p j h", p=P)
        for half in range(2):
            pair = slice(2 * half, 2 * half + 2)
            nc.sync.dma_start(out=w2_sb[:, pair], in_=w2_rows[:, pair])
        y_sb = keep.tile([P, ROW_TILES, N], BF16)
        nc.sync.dma_start(out=y_sb[:], in_=y.rearrange("(p r) n -> p r n", p=P))

        acc = {}

        def open_acc(j):
            acc[j] = psum.tile([P, N], F32, name="acc%d" % j)

        for j in (1, 2, 3):
            open_acc(j)

        def keep_tensor_busy(count):
            for i in range(count):
                nc.tensor.matmul(out=acc[3][:, 0:P], lhsT=ident[:], rhs=ident[:], start=True, stop=True)

        keep_tensor_busy(3)

        beta_abs = keep.tile([P, PASSES, PACK * N], BF16)
        beta_grouped = keep.tile([P, PASSES, N, PACK], BF16, align_bytes=64)
        sums_bank = psum.tile([P, N], F32)
        sums = sums_bank[:, 0 : COL_TILES * (PASSES + 1)].rearrange("p (j part) -> p j part", part=PASSES + 1)

        def clear_signs(g, first=0, last=PACK):
            pair = slice(first * N, last * N)
            nc.vector.tensor_scalar(
                out=beta_abs[:, g, pair].bitcast(I32),
                in0=beta_sb[:, g].rearrange("p t n -> p (t n)")[:, pair].bitcast(I32),
                scalar1=0x7FFF7FFF,
                scalar2=None,
                op0=ALU.bitwise_and,
            )

        def regroup(g):
            src = beta_sb[:, g].rearrange("p t (c i) -> p c t i", i=4)
            dst = beta_grouped[:, g].rearrange("p (c i) t -> p c t i", i=4)
            cut = VECTOR_COLS // 4
            nc.vector.tensor_copy(out=dst[:, :cut], in_=src[:, :cut])
            nc.scalar.copy(out=dst[:, cut:], in_=src[:, cut:])

        def sum_columns(g, busy_after_first=0):
            for j in range(COL_TILES):
                for t in range(PACK):
                    first = t * N + j * P
                    nc.tensor.matmul(
                        out=sums[:, j, g : g + 1],
                        lhsT=beta_abs[:, g, first : first + P],
                        rhs=ones[:],
                        start=(t == 0),
                        stop=(t == PACK - 1),
                    )
                    if j == 0 and t == 1:
                        keep_tensor_busy(busy_after_first)

        x_grouped = keep.tile([P, PASSES, B, PACK], BF16, align_bytes=64)
        x_grouped_words = x_grouped[:].rearrange("p g row t -> p (g row t)").bitcast(F32)
        x_grouped_words = x_grouped_words.rearrange("p (g row u) -> p g row u", g=PASSES, u=2)

        def transpose_x(r):
            words = x_sb[:, r].bitcast(F32)
            for g in range(PASSES):
                xt_bank = psum.tile([P, N], F32, name=(("xt0", "xt1"), ("norm_rows", "acc0"))[r][g])
                xt = xt_bank[:, 0 : 2 * P].rearrange("p (u row) -> p u row", u=2)
                for u in range(2):
                    nc.tensor.transpose(xt[:, u, :], words[:, 2 * g * P + u : 2 * (g + 1) * P : 2], ident[:])
                nc.scalar.copy(
                    out=x_grouped_words[:, g, r * P : (r + 1) * P], in_=xt.rearrange("p u row -> p row u")
                )

        beta_codes = keep.tile([P, PASSES, N], U32, align_bytes=64)
        beta_scales = keep.tile([P, PASSES, N], U8, align_bytes=64)
        x_codes = keep.tile([P, PASSES * B], U32, align_bytes=64)
        x_scales = keep.tile([P, PASSES * B], U8, align_bytes=64)

        def quantize_beta(g):
            nc.vector.quantize_mx(
                out=beta_codes[:, g].bitcast(FP8X4),
                scales=beta_scales[:, g],
                in_=beta_grouped[:, g].rearrange("p n t -> p (n t)"),
            )

        def keep_tensor_busy_mx(count):
            for i in range(count):
                nc.tensor.matmul_mx(
                    out=acc[3][:],
                    lhsT=beta_codes[:, 0, 0:P].bitcast(FP8X4),
                    lhsT_scale=beta_scales[:, 0, 0:P],
                    rhs=beta_codes[:, 0].bitcast(FP8X4),
                    rhs_scale=beta_scales[:, 0],
                    start=True,
                    stop=True,
                )

        bias_share = keep.tile([P, SCALAR_SUMS], F32)
        bias_sum = keep.tile([P, COL_TILES - SCALAR_SUMS], F32)
        summands = keep.tile([P, COL_TILES, NH], BF16)
        shift = keep.tile([P, COL_TILES], F32)

        def sum_biases_on_tensor():
            for part in range(2):
                nc.tensor.matmul(
                    out=sums[:, :, PASSES],
                    lhsT=bias_rows[:],
                    rhs=ident_bf[:, part * COL_TILES : (part + 1) * COL_TILES],
                    start=(part == 0),
                    stop=(part == 1),
                )

        def copy_biases_on_scalar():
            nc.scalar.activation(
                out=bias_share[:], in_=sums[:, 0:SCALAR_SUMS, PASSES], func=ACT.Copy, scale=1.0 / NH
            )
            nc.scalar.copy(out=bias_sum[:], in_=sums[:, SCALAR_SUMS:, PASSES])

        def sum_w2_on_vector(j):
            nc.vector.tensor_scalar(
                out=summands[:, j],
                in0=w2_sb[:, j],
                scalar1=float(NH),
                scalar2=bias_sum[:, j - SCALAR_SUMS : j - SCALAR_SUMS + 1],
                op0=ALU.mult,
                op1=ALU.add,
                accum_out=shift[:, j : j + 1],
            )

        def sum_w2(j):
            nc.scalar.activation(
                out=summands[:, j],
                in_=w2_sb[:, j],
                func=ACT.Identity,
                scale=float(NH),
                bias=bias_share[:, j : j + 1],
                accum_out=shift[:, j : j + 1],
            )

        clear_signs(0, 0, 2)
        clear_signs(0, 2, 4)
        regroup(0)
        sum_columns(0, busy_after_first=1)
        sum_biases_on_tensor()
        keep_tensor_busy(2)
        clear_signs(1)
        regroup(1)
        copy_biases_on_scalar()
        transpose_x(0)
        transpose_x(1)
        sum_columns(1)
        quantize_beta(0)
        quantize_beta(1)
        keep_tensor_busy_mx(2)
        norm = keep.tile([P, COL_TILES], F32)
        nc.vector.tensor_reduce(out=norm[:], in_=sums[:, :, 0:PASSES], axis=AXIS.X, op=ALU.add)
        norm_rows = psum.tile([P, N], F32)
        for j in range(COL_TILES):
            nc.tensor.transpose(
                norm_rows[:, j * P : (j + 1) * P],
                norm[:, j : j + 1].to_broadcast([P, P]),
                ident[:],
            )
        nc.vector.quantize_mx(
            out=x_codes[:].bitcast(FP8X4), scales=x_scales[:], in_=x_grouped[:].rearrange("p g row t -> p (g row t)")
        )
        for j in range(COL_TILES):
            if j < SCALAR_SUMS:
                sum_w2(j)
            else:
                sum_w2_on_vector(j)

        open_acc(0)
        for j in range(COL_TILES):
            for g in range(PASSES):
                cols = slice(j * P, (j + 1) * P)
                rows = slice(g * B, (g + 1) * B)
                nc.tensor.matmul_mx(
                    out=acc[j][:, 0:B],
                    lhsT=beta_codes[:, g, cols].bitcast(FP8X4),
                    lhsT_scale=beta_scales[:, g, cols],
                    rhs=x_codes[:, rows].bitcast(FP8X4),
                    rhs_scale=x_scales[:, rows],
                    start=(g == 0),
                    stop=(g == PASSES - 1),
                )

        total = keep.tile([P, ROW_TILES, N], F32)
        for half in range(2):
            cols = slice(half * N // 2, (half + 1) * N // 2)
            nc.vector.scalar_tensor_tensor(
                out=total[:, :, cols],
                in0=y_sb[:, :, cols],
                scalar=-EPSILON,
                in1=norm_rows[:, cols].unsqueeze(1).to_broadcast([P, ROW_TILES, N // 2]),
                op0=ALU.mult,
                op1=ALU.mult,
            )

        product = keep.tile([P, COL_TILES, B], F32)
        for j in range(COL_TILES):
            nc.scalar.activation(out=product[:, j], in_=acc[j][:, 0:B], func=ACT.Identity, bias=shift[:, j : j + 1])
        for j, bank in enumerate(("xt0", "xt1", "sums_bank", "acc0")):
            cols = slice(j * P, (j + 1) * P)
            bank_tile = psum.tile([P, N], F32, name=bank)
            product_rows = bank_tile[:, 0 : ROW_TILES * P].rearrange("p (r c) -> p r c", r=ROW_TILES)
            for r in range(ROW_TILES):
                nc.tensor.transpose(product_rows[:, r], product[:, j, r * P : (r + 1) * P], ident[:])
            nc.vector.tensor_tensor(
                out=total[:, :, cols], in0=total[:, :, cols], in1=product_rows, op=ALU.add
            )
            nc.sync.dma_start(out=out.rearrange("(p r) n -> p r n", p=P)[:, :, cols], in_=total[:, :, cols])
